import numpy as np
import ml_dtypes


def mxq(x, axis, fmt="e4m3"):
    dtype, down = {"e4m3": (ml_dtypes.float8_e4m3fn, 7), "e5m2": (ml_dtypes.float8_e5m2, 14)}[fmt]
    v = np.moveaxis(np.asarray(x, np.float32).astype(ml_dtypes.bfloat16).astype(np.float64), axis, -1)
    blocks = v.reshape(v.shape[:-1] + (-1, 32))
    amax = np.abs(blocks).max(-1, keepdims=True)
    byte = np.maximum(np.where(amax > 0, np.frexp(amax)[1] - 1 + 127, 0) - down, 1)
    scale = np.exp2(byte - 127.0)
    codes = (blocks / scale).astype(np.float32).astype(dtype).astype(np.float64)
    return np.moveaxis((codes * scale).reshape(v.shape), -1, axis)


WIDE = False


def mx_kscale(k):
    if not WIDE:
        return np.ones(k)
    levels = np.array([10, -10, 5, -5, 0])
    if k % 512:
        return np.exp2(np.random.permutation(np.resize(levels, k // 32))).repeat(32)
    a = np.empty((k // 512, 16))
    for p in range(k // 512):
        a[p, :8] = np.random.permutation(np.resize(levels, 8))
        for g in range(8):
            far = levels[np.abs(levels - a[p, g]) >= 10]
            a[p, g + 8] = far[np.random.randint(len(far))]
    return np.exp2(a.ravel()).repeat(32)


BF16 = ml_dtypes.bfloat16


def bf(x):
    return np.asarray(x, np.float32).astype(BF16)


def f64(x):
    return np.asarray(x).astype(np.float64)


B, T, N, C, WIN, F = 2, 6, 512, 512, 3, 2
NW = T - WIN + 1


def sigmoid(v):
    return 1.0 / (1.0 + np.exp(-v))


def setup_inputs():
    t = mx_kscale(C)
    return {"agg": bf(np.random.standard_normal((B, NW, N, C)) * t),
            "W": bf(np.random.standard_normal((NW, F, C, 2 * C)) / np.sqrt(C) / t[:, None]),
            "b": bf(np.random.standard_normal((NW, F, 2 * C)) * 0.3)}


def reference(agg, W, b):
    pre = (mxq(f64(agg), 3, "e4m3")[:, :, None] @ mxq(f64(W), 2, "e4m3")) + f64(b)[None, :, :, None, :]
    lhs, rhs = pre[..., :C], pre[..., C:]
    glu = lhs * sigmoid(rhs)
    return glu.max(axis=2)

@@ -1,0 +1,293 @@
+from contextlib import ExitStack
+
+import concourse.mybir as mybir
+from concourse.masks import make_identity
+
+F32 = mybir.dt.float32
+BF16 = mybir.dt.bfloat16
+U32 = mybir.dt.uint32
+U8 = mybir.dt.uint8
+FP8X4 = mybir.dt.float8_e4m3fn_x4
+ALU = mybir.AluOpType
+ACT = mybir.ActivationFunctionType
+
+P = 128
+FLOPS = 2 * 2 * 4 * 2 * 512 * 512 * 1024
+
+MANUAL = False
+CV = 576
+N_ROUNDS = 8
+
+
+def tile_stsindividuallayer_pb_t_kernel(tc, agg, W, b, out):
+    nc = tc.nc
+    with ExitStack() as ctx:
+        const = ctx.enter_context(tc.tile_pool(name="const", bufs=1))
+        rawp = ctx.enter_context(tc.tile_pool(name="raw", bufs=1))
+        wgp = ctx.enter_context(tc.tile_pool(name="wgp", bufs=2))
+        wqp = ctx.enter_context(tc.tile_pool(name="wqp", bufs=4))
+        agp = ctx.enter_context(tc.tile_pool(name="agp", bufs=2))
+        aqp = ctx.enter_context(tc.tile_pool(name="aqp", bufs=3))
+        sp = ctx.enter_context(tc.tile_pool(name="sp", bufs=4))
+        g0p = ctx.enter_context(tc.tile_pool(name="g0p", bufs=2))
+        g1p = ctx.enter_context(tc.tile_pool(name="g1p", bufs=3))
+        op = ctx.enter_context(tc.tile_pool(name="op", bufs=2))
+        psm = ctx.enter_context(tc.psum_pool(name="psm", bufs=6))
+        pst = ctx.enter_context(tc.psum_pool(name="pst", bufs=2))
+        if MANUAL:
+            ctx.enter_context(tc.manual_schedule())
+
+        araw = {}
+        wraw = {}
+        wgt = {}
+        wqt = {}
+        wst = {}
+        agt = {}
+        aqt = {}
+        ast = {}
+        xts = {}
+        rbs = {}
+        lbs = {}
+        sts = {}
+        g0t = {}
+        g1t = {}
+        obs = {}
+        ots = {}
+
+        def load_agg(r):
+            w, i = divmod(r, 2)
+            t = rawp.tile([P, 2048], BF16, name="araw%d" % r)
+            nc.sync.dma_start(out=t[:], in_=agg[i, w].rearrange("(p nt) k -> p (nt k)", nt=4))
+            araw[r] = t
+
+        def load_w(t_idx):
+            w, f = divmod(t_idx, 2)
+            t = rawp.tile([P, 4, 1024], BF16, name="wraw%d" % t_idx)
+            nc.sync.dma_start(
+                out=t[:].rearrange("q t c -> q (t c)"),
+                in_=W[w, f].rearrange("(q t) c -> q (t c)", t=4),
+            )
+            wraw[t_idx] = t
+
+        braw = const.tile([P, P], BF16, name="braw")
+        nc.scalar.dma_start(out=braw[0:64, :], in_=b.rearrange("w f (j c) -> (w f j) c", c=P))
+        load_agg(0)
+        load_w(0)
+        load_w(1)
+        load_agg(1)
+        for w in range(1, 4):
+            load_w(2 * w)
+            load_agg(2 * w)
+            load_w(2 * w + 1)
+            load_agg(2 * w + 1)
+
+        ident = const.tile([P, P], F32, name="ident")
+        make_identity(nc, ident[:])
+        zero1 = const.tile([P, 1], F32, name="zero1")
+        nc.vector.memset(zero1[:], 0.0)
+        warm = const.tile([P, 1], F32, name="warm")
+        nc.scalar.activation(out=warm[:], in_=zero1[:], func=ACT.Sigmoid)
+        bf32 = const.tile([P, P], F32, name="bf32")
+        nc.vector.memset(bf32[:], 0.0)
+        nc.vector.tensor_copy(out=bf32[0:64, :], in_=braw[0:64, :])
+        bias_sb = const.tile([P, 64], F32, name="bias_sb")
+
+        def agg_t(r, h):
+            xt = pst.tile([P, 512], F32, name="xt", tag="tp")
+            words = araw[r][:].bitcast(F32)
+            for u in range(2):
+                for a in range(2):
+                    nt = 2 * h + a
+                    nc.tensor.transpose(
+                        xt[:, 256 * u + 128 * a : 256 * u + 128 * a + 128],
+                        words[:, 256 * nt + u : 256 * nt + 256 : 2],
+                        ident[:],
+                    )
+            xts[(r, h)] = xt
+
+        def agg_copy(r, h):
+            if h == 0:
+                agt[r] = agp.tile([P, 1024], F32, name="ag", tag="ag", align_bytes=64)
+            nc.scalar.copy(
+                out=agt[r][:, 512 * h : 512 * h + 512].rearrange("p (n u) -> p n u", u=2),
+                in_=xts[(r, h)][:].rearrange("p (u n) -> p n u", u=2),
+            )
+
+        def agg_q(r):
+            aqt[r] = aqp.tile([P, 512], U32, name="aq", tag="aq", align_bytes=64)
+            ast[r] = aqp.tile([P, 512], U8, name="asc", tag="asc", align_bytes=64)
+            nc.vector.quantize_mx(
+                out=aqt[r][:].bitcast(FP8X4), scales=ast[r][:], in_=agt[r][:].bitcast(BF16)
+            )
+
+        def regroup(t_idx, c0, c1, on_vector):
+            if t_idx not in wgt:
+                wgt[t_idx] = wgp.tile([P, 1024, 4], BF16, name="wg", tag="wg", align_bytes=64)
+            dst = wgt[t_idx][:, c0:c1, :].rearrange("p (c i) t -> p c t i", i=4)
+            src = wraw[t_idx][:, :, c0:c1].rearrange("p t (c i) -> p c t i", i=4)
+            if on_vector:
+                nc.vector.tensor_copy(out=dst, in_=src)
+            else:
+                nc.scalar.copy(out=dst, in_=src)
+
+        def w_q(t_idx):
+            wqt[t_idx] = wqp.tile([P, 1024], U32, name="wq", tag="wq", align_bytes=64)
+            wst[t_idx] = wqp.tile([P, 1024], U8, name="wsc", tag="wsc", align_bytes=64)
+            nc.vector.quantize_mx(
+                out=wqt[t_idx][:].bitcast(FP8X4),
+                scales=wst[t_idx][:],
+                in_=wgt[t_idx][:].rearrange("p c t -> p (c t)"),
+            )
+
+        def unit(uu):
+            r, u = divmod(uu, 8)
+            f, cb = divmod(u, 4)
+            return r, f, cb, 2 * (r // 2) + f
+
+        def one_pass(acc, t_idx, j, r):
+            nc.tensor.matmul_mx(
+                out=acc[:],
+                lhsT=wqt[t_idx][:, 128 * j : 128 * j + 128].bitcast(FP8X4),
+                lhsT_scale=wst[t_idx][:, 128 * j : 128 * j + 128],
+                rhs=aqt[r][:].bitcast(FP8X4),
+                rhs_scale=ast[r][:],
+                start=True,
+                stop=True,
+            )
+
+        def mx(uu):
+            r, f, cb, t_idx = unit(uu)
+            rbs[uu] = psm.tile([P, 512], F32, name="rb", tag="mx")
+            one_pass(rbs[uu], t_idx, 4 + cb, r)
+            lbs[uu] = psm.tile([P, 512], F32, name="lb", tag="mx")
+            one_pass(lbs[uu], t_idx, cb, r)
+
+        def sig(uu):
+            r, f, cb, t_idx = unit(uu)
+            col = 8 * t_idx + 4 + cb
+            sts[uu] = sp.tile([P, 512], F32, name="s", tag="s")
+            nc.scalar.activation(
+                out=sts[uu][:], in_=rbs[uu][:], func=ACT.Sigmoid, bias=bias_sb[:, col : col + 1], scale=1.0
+            )
+
+        def stt(uu):
+            r, f, cb, t_idx = unit(uu)
+            col = 8 * t_idx + cb
+            if f == 0:
+                if cb == 0:
+                    g0t[r] = g0p.tile([P, 4, 512], F32, name="g0", tag="g0")
+                dst = g0t[r][:, cb, :]
+            else:
+                g1t[(r, cb)] = g1p.tile([P, 512], F32, name="g1", tag="g1")
+                dst = g1t[(r, cb)][:]
+            nc.vector.scalar_tensor_tensor(
+                out=dst,
+                in0=lbs[uu][:],
+                scalar=bias_sb[:, col : col + 1],
+                in1=sts[uu][:],
+                op0=ALU.add,
+                op1=ALU.mult,
+            )
+
+        def vmax(r, cb):
+            nc.vector.tensor_tensor(
+                out=g0t[r][:, cb, :], in0=g0t[r][:, cb, :], in1=g1t[(r, cb)][:], op=ALU.max
+            )
+
+        def out_t(r, nt, big):
+            if big:
+                ob = psm.tile([P, 512], F32, name="ob2", tag="mx")
+            else:
+                ob = pst.tile([P, 512], F32, name="ob", tag="tp")
+            for cb in range(4):
+                nc.tensor.transpose(
+                    ob[:, 128 * cb : 128 * cb + 128], g0t[r][:, cb, 128 * nt : 128 * nt + 128], ident[:]
+                )
+            obs[(r, nt)] = ob
+
+        def out_copy(r, nt, on_vector):
+            if nt == 0:
+                ots[r] = op.tile([P, 4, 512], F32, name="o", tag="o")
+            if on_vector:
+                nc.vector.tensor_copy(out=ots[r][:, nt, :], in_=obs[(r, nt)][:])
+            else:
+                nc.scalar.copy(out=ots[r][:, nt, :], in_=obs[(r, nt)][:])
+
+        def store(r, n0, n1):
+            w, i = divmod(r, 2)
+            nc.sync.dma_start(
+                out=out[i, w].rearrange("(p nt) c -> p nt c", nt=4)[:, n0:n1, :], in_=ots[r][:, n0:n1, :]
+            )
+
+        hv = CV // 2
+        hs = (1024 - CV) // 2
+
+        agg_t(0, 0)
+        agg_t(0, 1)
+        bt = psm.tile([P, 512], F32, name="bt", tag="mx")
+        nc.tensor.transpose(bt[:, 0:128], bf32[:], ident[:])
+        nc.vector.tensor_copy(out=bias_sb[:], in_=bt[:, 0:64])
+        agg_copy(0, 0)
+        agg_copy(0, 1)
+        regroup(0, 0, CV, True)
+        regroup(0, CV, 1024, False)
+        agg_q(0)
+        w_q(0)
+        regroup(1, 0, CV, True)
+        regroup(1, CV, 1024, False)
+        mx(0)
+        mx(1)
+
+        for r in range(N_ROUNDS):
+            for u in range(8):
+                uu = 8 * r + u
+                if uu + 2 < 8 * N_ROUNDS:
+                    mx(uu + 2)
+                if u == 0 and r + 1 < N_ROUNDS:
+                    agg_t(r + 1, 0)
+                    agg_t(r + 1, 1)
+                if r >= 1:
+                    if u == 3:
+                        out_t(r - 1, 0, False)
+                        out_t(r - 1, 1, False)
+                    if u == 5:
+                        out_t(r - 1, 2, False)
+                    if u == 6:
+                        out_t(r - 1, 3, False)
+                sig(uu)
+                if u == 0 and r + 2 < 8:
+                    regroup(r + 2, CV, CV + hs, False)
+                if u in (1, 2) and r + 1 < N_ROUNDS:
+                    agg_copy(r + 1, u - 1)
+                if u == 3 and r + 2 < 8:
+                    regroup(r + 2, CV + hs, 1024, False)
+                if u >= 4 and r >= 1:
+                    out_copy(r - 1, u - 4, False)
+                    if u == 7:
+                        store(r - 1, 0, 4)
+                stt(uu)
+                if u == 0 and r + 1 < 8:
+                    w_q(r + 1)
+                if u == 1 and r >= 1:
+                    vmax(r - 1, 3)
+                if u == 2 and r + 2 < 8:
+                    regroup(r + 2, 0, hv, True)
+                if u == 3 and r + 2 < 8:
+                    regroup(r + 2, hv, CV, True)
+                if u == 4 and r + 1 < N_ROUNDS:
+                    agg_q(r + 1)
+                if u >= 5:
+                    vmax(r, u - 5)
+
+        last = N_ROUNDS - 1
+        vmax(last, 3)
+        out_t(last, 0, False)
+        out_t(last, 1, False)
+        out_t(last, 2, True)
+        out_t(last, 3, True)
+        out_copy(last, 0, False)
+        out_copy(last, 1, True)
+        store(last, 0, 2)
+        out_copy(last, 2, False)
+        out_copy(last, 3, True)
+        store(last, 2, 4)

@@ -14,9 +14,9 @@ ACT = mybir.ActivationFunctionType
 P = 128
 FLOPS = 2 * 2 * 4 * 2 * 512 * 512 * 1024
 
-MANUAL = False
 CV = 576
 N_ROUNDS = 8
+LEAD = 2
 
 
 def tile_stsindividuallayer_pb_t_kernel(tc, agg, W, b, out):
@@ -28,14 +28,15 @@ def tile_stsindividuallayer_pb_t_kernel(tc, agg, W, b, out):
         wqp = ctx.enter_context(tc.tile_pool(name="wqp", bufs=4))
         agp = ctx.enter_context(tc.tile_pool(name="agp", bufs=2))
         aqp = ctx.enter_context(tc.tile_pool(name="aqp", bufs=3))
-        sp = ctx.enter_context(tc.tile_pool(name="sp", bufs=4))
+        sp = ctx.enter_context(tc.tile_pool(name="sp", bufs=6))
         g0p = ctx.enter_context(tc.tile_pool(name="g0p", bufs=2))
         g1p = ctx.enter_context(tc.tile_pool(name="g1p", bufs=3))
         op = ctx.enter_context(tc.tile_pool(name="op", bufs=2))
-        psm = ctx.enter_context(tc.psum_pool(name="psm", bufs=6))
+        psr = ctx.enter_context(tc.psum_pool(name="psr", bufs=2))
+        psl = ctx.enter_context(tc.psum_pool(name="psl", bufs=4))
         pst = ctx.enter_context(tc.psum_pool(name="pst", bufs=2))
-        if MANUAL:
-            ctx.enter_context(tc.manual_schedule())
+
+        ctx.enter_context(tc.manual_schedule())
 
         araw = {}
         wraw = {}
@@ -155,14 +156,21 @@ def tile_stsindividuallayer_pb_t_kernel(tc, agg, W, b, out):
                 stop=True,
             )
 
-        def mx(uu):
-            r, f, cb, t_idx = unit(uu)
-            rbs[uu] = psm.tile([P, 512], F32, name="rb", tag="mx")
-            one_pass(rbs[uu], t_idx, 4 + cb, r)
-            lbs[uu] = psm.tile([P, 512], F32, name="lb", tag="mx")
-            one_pass(lbs[uu], t_idx, cb, r)
+        def mx_gate(uu):
+            if uu < 8 * N_ROUNDS:
+                r, f, cb, t_idx = unit(uu)
+                rbs[uu] = psr.tile([P, 512], F32, name="rb", tag="rb")
+                one_pass(rbs[uu], t_idx, 4 + cb, r)
+
+        def mx_value(uu):
+            if uu < 8 * N_ROUNDS:
+                r, f, cb, t_idx = unit(uu)
+                lbs[uu] = psl.tile([P, 512], F32, name="lb", tag="lb")
+                one_pass(lbs[uu], t_idx, cb, r)
 
         def sig(uu):
+            if uu >= 8 * N_ROUNDS:
+                return
             r, f, cb, t_idx = unit(uu)
             col = 8 * t_idx + 4 + cb
             sts[uu] = sp.tile([P, 512], F32, name="s", tag="s")
@@ -196,7 +204,7 @@ def tile_stsindividuallayer_pb_t_kernel(tc, agg, W, b, out):
 
         def out_t(r, nt, big):
             if big:
-                ob = psm.tile([P, 512], F32, name="ob2", tag="mx")
+                ob = psl.tile([P, 512], F32, name="ob2", tag="lb")
             else:
                 ob = pst.tile([P, 512], F32, name="ob", tag="tp")
             for cb in range(4):
@@ -224,7 +232,7 @@ def tile_stsindividuallayer_pb_t_kernel(tc, agg, W, b, out):
 
         agg_t(0, 0)
         agg_t(0, 1)
-        bt = psm.tile([P, 512], F32, name="bt", tag="mx")
+        bt = psl.tile([P, 512], F32, name="bt", tag="lb")
         nc.tensor.transpose(bt[:, 0:128], bf32[:], ident[:])
         nc.vector.tensor_copy(out=bias_sb[:], in_=bt[:, 0:64])
         agg_copy(0, 0)
@@ -235,14 +243,21 @@ def tile_stsindividuallayer_pb_t_kernel(tc, agg, W, b, out):
         w_q(0)
         regroup(1, 0, CV, True)
         regroup(1, CV, 1024, False)
-        mx(0)
-        mx(1)
+        for k in range(LEAD + 2):
+            mx_gate(k)
+            if k < 3:
+                mx_value(k)
+            if k < LEAD:
+                sig(k)
 
         for r in range(N_ROUNDS):
             for u in range(8):
                 uu = 8 * r + u
-                if uu + 2 < 8 * N_ROUNDS:
-                    mx(uu + 2)
+                if u == 0 and r + 1 < 8:
+                    w_q(r + 1)
+                if u == 4 and r + 1 < N_ROUNDS:
+                    agg_q(r + 1)
+                mx_value(uu + 3)
                 if u == 0 and r + 1 < N_ROUNDS:
                     agg_t(r + 1, 0)
                     agg_t(r + 1, 1)
@@ -254,7 +269,8 @@ def tile_stsindividuallayer_pb_t_kernel(tc, agg, W, b, out):
                         out_t(r - 1, 2, False)
                     if u == 6:
                         out_t(r - 1, 3, False)
-                sig(uu)
+                sig(uu + LEAD)
+                mx_gate(uu + LEAD + 2)
                 if u == 0 and r + 2 < 8:
                     regroup(r + 2, CV, CV + hs, False)
                 if u in (1, 2) and r + 1 < N_ROUNDS:
@@ -266,16 +282,12 @@ def tile_stsindividuallayer_pb_t_kernel(tc, agg, W, b, out):
                     if u == 7:
                         store(r - 1, 0, 4)
                 stt(uu)
-                if u == 0 and r + 1 < 8:
-                    w_q(r + 1)
                 if u == 1 and r >= 1:
                     vmax(r - 1, 3)
                 if u == 2 and r + 2 < 8:
                     regroup(r + 2, 0, hv, True)
                 if u == 3 and r + 2 < 8:
                     regroup(r + 2, hv, CV, True)
-                if u == 4 and r + 1 < N_ROUNDS:
-                    agg_q(r + 1)
                 if u >= 5:
                     vmax(r, u - 5)
 

@@ -14,7 +14,7 @@ ACT = mybir.ActivationFunctionType
 P = 128
 FLOPS = 2 * 2 * 4 * 2 * 512 * 512 * 1024
 
-CV = 576
+CV = 608
 N_ROUNDS = 8
 LEAD = 2
 
@@ -40,6 +40,7 @@ def tile_stsindividuallayer_pb_t_kernel(tc, agg, W, b, out):
 
         araw = {}
         wraw = {}
+        w0raw = {}
         wgt = {}
         wqt = {}
         wst = {}
@@ -70,10 +71,18 @@ def tile_stsindividuallayer_pb_t_kernel(tc, agg, W, b, out):
             )
             wraw[t_idx] = t
 
+        def load_w0(half):
+            t = rawp.tile([P, 4, 512], BF16, name="wraw0_%d" % half)
+            nc.sync.dma_start(
+                out=t[:], in_=W[0, 0].rearrange("(q t) c -> q t c", t=4)[:, :, 512 * half : 512 * half + 512]
+            )
+            w0raw[half] = t
+
         braw = const.tile([P, P], BF16, name="braw")
         nc.scalar.dma_start(out=braw[0:64, :], in_=b.rearrange("w f (j c) -> (w f j) c", c=P))
+        load_w0(1)
+        load_w0(0)
         load_agg(0)
-        load_w(0)
         load_w(1)
         load_agg(1)
         for w in range(1, 4):
@@ -125,19 +134,24 @@ def tile_stsindividuallayer_pb_t_kernel(tc, agg, W, b, out):
             if t_idx not in wgt:
                 wgt[t_idx] = wgp.tile([P, 1024, 4], BF16, name="wg", tag="wg", align_bytes=64)
             dst = wgt[t_idx][:, c0:c1, :].rearrange("p (c i) t -> p c t i", i=4)
-            src = wraw[t_idx][:, :, c0:c1].rearrange("p t (c i) -> p c t i", i=4)
+            if t_idx == 0:
+                half = c0 // 512
+                src = w0raw[half][:, :, c0 - 512 * half : c1 - 512 * half].rearrange("p t (c i) -> p c t i", i=4)
+            else:
+                src = wraw[t_idx][:, :, c0:c1].rearrange("p t (c i) -> p c t i", i=4)
             if on_vector:
                 nc.vector.tensor_copy(out=dst, in_=src)
             else:
                 nc.scalar.copy(out=dst, in_=src)
 
-        def w_q(t_idx):
-            wqt[t_idx] = wqp.tile([P, 1024], U32, name="wq", tag="wq", align_bytes=64)
-            wst[t_idx] = wqp.tile([P, 1024], U8, name="wsc", tag="wsc", align_bytes=64)
+        def w_q(t_idx, c0=0, c1=1024):
+            if t_idx not in wqt:
+                wqt[t_idx] = wqp.tile([P, 1024], U32, name="wq", tag="wq", align_bytes=64)
+                wst[t_idx] = wqp.tile([P, 1024], U8, name="wsc", tag="wsc", align_bytes=64)
             nc.vector.quantize_mx(
-                out=wqt[t_idx][:].bitcast(FP8X4),
-                scales=wst[t_idx][:],
-                in_=wgt[t_idx][:].rearrange("p c t -> p (c t)"),
+                out=wqt[t_idx][:, c0:c1].bitcast(FP8X4),
+                scales=wst[t_idx][:, c0:c1],
+                in_=wgt[t_idx][:, c0:c1, :].rearrange("p c t -> p (c t)"),
             )
 
         def unit(uu):
@@ -221,6 +235,32 @@ def tile_stsindividuallayer_pb_t_kernel(tc, agg, W, b, out):
             else:
                 nc.scalar.copy(out=ots[r][:, nt, :], in_=obs[(r, nt)][:])
 
+        def out_t_cb(cb):
+            if cb < 2:
+                ob = pst.tile([P, 4, P], F32, name="oc", tag="tp")
+            else:
+                ob = psr.tile([P, 4, P], F32, name="oc", tag="rb")
+            for nt in range(4):
+                nc.tensor.transpose(ob[:, nt, :], g0t[7][:, cb, P * nt : P * nt + P], ident[:])
+            obs[cb] = ob
+
+        def out_copy_cb(cb, n0, n1, on_vector):
+            half, part = divmod(cb, 2)
+            if part == 0 and n0 == 0:
+                ots[(7, half)] = op.tile([P, 4, 256], F32, name="oh", tag="oh")
+            dst = ots[(7, half)][:, n0:n1, P * part : P * part + P]
+            src = obs[cb][:, n0:n1, :]
+            if on_vector:
+                nc.vector.tensor_copy(out=dst, in_=src)
+            else:
+                nc.scalar.copy(out=dst, in_=src)
+
+        def store_half(half):
+            nc.sync.dma_start(
+                out=out[1, 3].rearrange("(p nt) c -> p nt c", nt=4)[:, :, 256 * half : 256 * half + 256],
+                in_=ots[(7, half)][:],
+            )
+
         def store(r, n0, n1):
             w, i = divmod(r, 2)
             nc.sync.dma_start(
@@ -230,19 +270,22 @@ def tile_stsindividuallayer_pb_t_kernel(tc, agg, W, b, out):
         hv = CV // 2
         hs = (1024 - CV) // 2
 
+        regroup(0, 512, 832, True)
+        regroup(0, 832, 1024, False)
+        regroup(0, 0, 320, True)
+        regroup(0, 320, 512, False)
+        w_q(0, 512, 1024)
         agg_t(0, 0)
         agg_t(0, 1)
+        w_q(0, 0, 512)
+        agg_copy(0, 0)
+        agg_copy(0, 1)
         bt = psl.tile([P, 512], F32, name="bt", tag="lb")
         nc.tensor.transpose(bt[:, 0:128], bf32[:], ident[:])
         nc.vector.tensor_copy(out=bias_sb[:], in_=bt[:, 0:64])
-        agg_copy(0, 0)
-        agg_copy(0, 1)
-        regroup(0, 0, CV, True)
-        regroup(0, CV, 1024, False)
         agg_q(0)
-        w_q(0)
-        regroup(1, 0, CV, True)
-        regroup(1, CV, 1024, False)
+        regroup(1, 0, 768, True)
+        regroup(1, 768, 1024, False)
         for k in range(LEAD + 2):
             mx_gate(k)
             if k < 3:
@@ -251,9 +294,10 @@ def tile_stsindividuallayer_pb_t_kernel(tc, agg, W, b, out):
                 sig(k)
 
         for r in range(N_ROUNDS):
+            first = 4 if r < N_ROUNDS - 1 else 2
             for u in range(8):
                 uu = 8 * r + u
-                if u == 0 and r + 1 < 8:
+                if u == 0 and 1 <= r < 7:
                     w_q(r + 1)
                 if u == 4 and r + 1 < N_ROUNDS:
                     agg_q(r + 1)
@@ -262,27 +306,33 @@ def tile_stsindividuallayer_pb_t_kernel(tc, agg, W, b, out):
                     agg_t(r + 1, 0)
                     agg_t(r + 1, 1)
                 if r >= 1:
-                    if u == 3:
+                    if u == first - 1:
                         out_t(r - 1, 0, False)
                         out_t(r - 1, 1, False)
-                    if u == 5:
+                    if u == first + 1:
                         out_t(r - 1, 2, False)
-                    if u == 6:
+                    if u == first + 2:
                         out_t(r - 1, 3, False)
                 sig(uu + LEAD)
-                mx_gate(uu + LEAD + 2)
+                if uu > 0:
+                    mx_gate(uu + LEAD + 2)
                 if u == 0 and r + 2 < 8:
                     regroup(r + 2, CV, CV + hs, False)
                 if u in (1, 2) and r + 1 < N_ROUNDS:
                     agg_copy(r + 1, u - 1)
                 if u == 3 and r + 2 < 8:
                     regroup(r + 2, CV + hs, 1024, False)
-                if u >= 4 and r >= 1:
-                    out_copy(r - 1, u - 4, False)
-                    if u == 7:
-                        store(r - 1, 0, 4)
+                if first <= u < first + 4 and r >= 1:
+                    out_copy(r - 1, u - first, False)
+                    if u == first + 1:
+                        store(r - 1, 0, 2)
+                    if u == first + 3:
+                        store(r - 1, 2, 4)
                 stt(uu)
-                if u == 1 and r >= 1:
+                if uu == 0:
+                    w_q(1)
+                    mx_gate(LEAD + 2)
+                if u == (1 if r < N_ROUNDS - 1 else 0) and r >= 1:
                     vmax(r - 1, 3)
                 if u == 2 and r + 2 < 8:
                     regroup(r + 2, 0, hv, True)
@@ -290,16 +340,16 @@ def tile_stsindividuallayer_pb_t_kernel(tc, agg, W, b, out):
                     regroup(r + 2, hv, CV, True)
                 if u >= 5:
                     vmax(r, u - 5)
+                    if r == N_ROUNDS - 1:
+                        out_t_cb(u - 5)
+                        if u > 5:
+                            out_copy_cb(u - 6, 0, 4, False)
 
-        last = N_ROUNDS - 1
-        vmax(last, 3)
-        out_t(last, 0, False)
-        out_t(last, 1, False)
-        out_t(last, 2, True)
-        out_t(last, 3, True)
-        out_copy(last, 0, False)
-        out_copy(last, 1, True)
-        store(last, 0, 2)
-        out_copy(last, 2, False)
-        out_copy(last, 3, True)
-        store(last, 2, 4)
+        vmax(7, 3)
+        store_half(0)
+        out_t_cb(3)
+        out_copy_cb(2, 0, 2, True)
+        out_copy_cb(2, 2, 4, False)
+        out_copy_cb(3, 0, 2, True)
+        out_copy_cb(3, 2, 4, False)
+        store_half(1)

@@ -14,7 +14,8 @@ ACT = mybir.ActivationFunctionType
 P = 128
 FLOPS = 2 * 2 * 4 * 2 * 512 * 512 * 1024
 
-CV = 608
+CV = 464
+GC = 256
 N_ROUNDS = 8
 LEAD = 2
 
@@ -144,6 +145,17 @@ def tile_stsindividuallayer_pb_t_kernel(tc, agg, W, b, out):
             else:
                 nc.scalar.copy(out=dst, in_=src)
 
+        def regroup_g(t_idx):
+            wgt[t_idx] = wgp.tile([P, 1024, 4], BF16, name="wg", tag="wg", align_bytes=64)
+            nc.gpsimd.tensor_scalar(
+                out=wgt[t_idx][:, 1024 - GC : 1024, :],
+                in0=wraw[t_idx][:, :, 1024 - GC : 1024].rearrange("p t c -> p c t"),
+                scalar1=1.0,
+                scalar2=0.0,
+                op0=ALU.mult,
+                op1=ALU.add,
+            )
+
         def w_q(t_idx, c0=0, c1=1024):
             if t_idx not in wqt:
                 wqt[t_idx] = wqp.tile([P, 1024], U32, name="wq", tag="wq", align_bytes=64)
@@ -267,8 +279,6 @@ def tile_stsindividuallayer_pb_t_kernel(tc, agg, W, b, out):
                 out=out[i, w].rearrange("(p nt) c -> p nt c", nt=4)[:, n0:n1, :], in_=ots[r][:, n0:n1, :]
             )
 
-        hv = CV // 2
-        hs = (1024 - CV) // 2
 
         regroup(0, 512, 832, True)
         regroup(0, 832, 1024, False)
@@ -294,11 +304,18 @@ def tile_stsindividuallayer_pb_t_kernel(tc, agg, W, b, out):
                 sig(k)
 
         for r in range(N_ROUNDS):
+            cv, end = (608, 1024) if r < 2 else (CV, 1024 - GC)
             first = 4 if r < N_ROUNDS - 1 else 2
             for u in range(8):
                 uu = 8 * r + u
+                if u == 0 and r >= 1:
+                    vmax(r - 1, 3)
                 if u == 0 and 1 <= r < 7:
                     w_q(r + 1)
+                    if r == 1:
+                        regroup(3, cv, (cv + end) // 2, False)
+                    if r + 3 < 8:
+                        regroup_g(r + 3)
                 if u == 4 and r + 1 < N_ROUNDS:
                     agg_q(r + 1)
                 mx_value(uu + 3)
@@ -316,12 +333,12 @@ def tile_stsindividuallayer_pb_t_kernel(tc, agg, W, b, out):
                 sig(uu + LEAD)
                 if uu > 0:
                     mx_gate(uu + LEAD + 2)
-                if u == 0 and r + 2 < 8:
-                    regroup(r + 2, CV, CV + hs, False)
+                if u == 0 and r + 2 < 8 and r != 1:
+                    regroup(r + 2, cv, (cv + end) // 2, False)
                 if u in (1, 2) and r + 1 < N_ROUNDS:
                     agg_copy(r + 1, u - 1)
                 if u == 3 and r + 2 < 8:
-                    regroup(r + 2, CV + hs, 1024, False)
+                    regroup(r + 2, (cv + end) // 2, end, False)
                 if first <= u < first + 4 and r >= 1:
                     out_copy(r - 1, u - first, False)
                     if u == first + 1:
@@ -332,12 +349,10 @@ def tile_stsindividuallayer_pb_t_kernel(tc, agg, W, b, out):
                 if uu == 0:
                     w_q(1)
                     mx_gate(LEAD + 2)
-                if u == (1 if r < N_ROUNDS - 1 else 0) and r >= 1:
-                    vmax(r - 1, 3)
-                if u == 2 and r + 2 < 8:
-                    regroup(r + 2, 0, hv, True)
-                if u == 3 and r + 2 < 8:
-                    regroup(r + 2, hv, CV, True)
+                if u == (2 if r == 0 else 3) and r + 2 < 8:
+                    regroup(r + 2, 0, cv // 2, True)
+                if u == (3 if r == 0 else 4) and r + 2 < 8:
+                    regroup(r + 2, cv // 2, cv, True)
                 if u >= 5:
                     vmax(r, u - 5)
                     if r == N_ROUNDS - 1:

from contextlib import ExitStack

import concourse.mybir as mybir
from concourse.masks import make_identity

F32 = mybir.dt.float32
BF16 = mybir.dt.bfloat16
U32 = mybir.dt.uint32
U8 = mybir.dt.uint8
FP8X4 = mybir.dt.float8_e4m3fn_x4
ALU = mybir.AluOpType
ACT = mybir.ActivationFunctionType

P = 128
FLOPS = 2 * 2 * 4 * 2 * 512 * 512 * 1024

CV = 464
GC = 256
N_ROUNDS = 8
LEAD = 2


def tile_stsindividuallayer_pb_t_kernel(tc, agg, W, b, out):
    nc = tc.nc
    with ExitStack() as ctx:
        const = ctx.enter_context(tc.tile_pool(name="const", bufs=1))
        rawp = ctx.enter_context(tc.tile_pool(name="raw", bufs=1))
        wgp = ctx.enter_context(tc.tile_pool(name="wgp", bufs=2))
        wqp = ctx.enter_context(tc.tile_pool(name="wqp", bufs=4))
        agp = ctx.enter_context(tc.tile_pool(name="agp", bufs=2))
        aqp = ctx.enter_context(tc.tile_pool(name="aqp", bufs=3))
        sp = ctx.enter_context(tc.tile_pool(name="sp", bufs=6))
        g0p = ctx.enter_context(tc.tile_pool(name="g0p", bufs=2))
        g1p = ctx.enter_context(tc.tile_pool(name="g1p", bufs=3))
        op = ctx.enter_context(tc.tile_pool(name="op", bufs=2))
        psr = ctx.enter_context(tc.psum_pool(name="psr", bufs=2))
        psl = ctx.enter_context(tc.psum_pool(name="psl", bufs=4))
        pst = ctx.enter_context(tc.psum_pool(name="pst", bufs=2))

        ctx.enter_context(tc.manual_schedule())

        araw = {}
        wraw = {}
        w0raw = {}
        wgt = {}
        wqt = {}
        wst = {}
        agt = {}
        aqt = {}
        ast = {}
        xts = {}
        rbs = {}
        lbs = {}
        sts = {}
        g0t = {}
        g1t = {}
        obs = {}
        ots = {}

        def load_agg(r):
            w, i = divmod(r, 2)
            t = rawp.tile([P, 2048], BF16, name="araw%d" % r)
            nc.sync.dma_start(out=t[:], in_=agg[i, w].rearrange("(p nt) k -> p (nt k)", nt=4))
            araw[r] = t

        def load_w(t_idx):
            w, f = divmod(t_idx, 2)
            t = rawp.tile([P, 4, 1024], BF16, name="wraw%d" % t_idx)
            nc.sync.dma_start(
                out=t[:].rearrange("q t c -> q (t c)"),
                in_=W[w, f].rearrange("(q t) c -> q (t c)", t=4),
            )
            wraw[t_idx] = t

        def load_w0(half):
            t = rawp.tile([P, 4, 512], BF16, name="wraw0_%d" % half)
            nc.sync.dma_start(
                out=t[:], in_=W[0, 0].rearrange("(q t) c -> q t c", t=4)[:, :, 512 * half : 512 * half + 512]
            )
            w0raw[half] = t

        braw = const.tile([P, P], BF16, name="braw")
        nc.scalar.dma_start(out=braw[0:64, :], in_=b.rearrange("w f (j c) -> (w f j) c", c=P))
        load_w0(1)
        load_w0(0)
        load_agg(0)
        load_w(1)
        load_agg(1)
        for w in range(1, 4):
            load_w(2 * w)
            load_agg(2 * w)
            load_w(2 * w + 1)
            load_agg(2 * w + 1)

        ident = const.tile([P, P], F32, name="ident")
        make_identity(nc, ident[:])
        zero1 = const.tile([P, 1], F32, name="zero1")
        nc.vector.memset(zero1[:], 0.0)
        warm = const.tile([P, 1], F32, name="warm")
        nc.scalar.activation(out=warm[:], in_=zero1[:], func=ACT.Sigmoid)
        bf32 = const.tile([P, P], F32, name="bf32")
        nc.vector.memset(bf32[:], 0.0)
        nc.vector.tensor_copy(out=bf32[0:64, :], in_=braw[0:64, :])
        bias_sb = const.tile([P, 64], F32, name="bias_sb")

        def agg_t(r, h):
            xt = pst.tile([P, 512], F32, name="xt", tag="tp")
            words = araw[r][:].bitcast(F32)
            for u in range(2):
                for a in range(2):
                    nt = 2 * h + a
                    nc.tensor.transpose(
                        xt[:, 256 * u + 128 * a : 256 * u + 128 * a + 128],
                        words[:, 256 * nt + u : 256 * nt + 256 : 2],
                        ident[:],
                    )
            xts[(r, h)] = xt

        def agg_copy(r, h):
            if h == 0:
                agt[r] = agp.tile([P, 1024], F32, name="ag", tag="ag", align_bytes=64)
            nc.scalar.copy(
                out=agt[r][:, 512 * h : 512 * h + 512].rearrange("p (n u) -> p n u", u=2),
                in_=xts[(r, h)][:].rearrange("p (u n) -> p n u", u=2),
            )

        def agg_q(r):
            aqt[r] = aqp.tile([P, 512], U32, name="aq", tag="aq", align_bytes=64)
            ast[r] = aqp.tile([P, 512], U8, name="asc", tag="asc", align_bytes=64)
            nc.vector.quantize_mx(
                out=aqt[r][:].bitcast(FP8X4), scales=ast[r][:], in_=agt[r][:].bitcast(BF16)
            )

        def regroup(t_idx, c0, c1, on_vector):
            if t_idx not in wgt:
                wgt[t_idx] = wgp.tile([P, 1024, 4], BF16, name="wg", tag="wg", align_bytes=64)
            dst = wgt[t_idx][:, c0:c1, :].rearrange("p (c i) t -> p c t i", i=4)
            if t_idx == 0:
                half = c0 // 512
                src = w0raw[half][:, :, c0 - 512 * half : c1 - 512 * half].rearrange("p t (c i) -> p c t i", i=4)
            else:
                src = wraw[t_idx][:, :, c0:c1].rearrange("p t (c i) -> p c t i", i=4)
            if on_vector:
                nc.vector.tensor_copy(out=dst, in_=src)
            else:
                nc.scalar.copy(out=dst, in_=src)

        def regroup_g(t_idx):
            wgt[t_idx] = wgp.tile([P, 1024, 4], BF16, name="wg", tag="wg", align_bytes=64)
            nc.gpsimd.tensor_scalar(
                out=wgt[t_idx][:, 1024 - GC : 1024, :],
                in0=wraw[t_idx][:, :, 1024 - GC : 1024].rearrange("p t c -> p c t"),
                scalar1=1.0,
                scalar2=0.0,
                op0=ALU.mult,
                op1=ALU.add,
            )

        def w_q(t_idx, c0=0, c1=1024):
            if t_idx not in wqt:
                wqt[t_idx] = wqp.tile([P, 1024], U32, name="wq", tag="wq", align_bytes=64)
                wst[t_idx] = wqp.tile([P, 1024], U8, name="wsc", tag="wsc", align_bytes=64)
            nc.vector.quantize_mx(
                out=wqt[t_idx][:, c0:c1].bitcast(FP8X4),
                scales=wst[t_idx][:, c0:c1],
                in_=wgt[t_idx][:, c0:c1, :].rearrange("p c t -> p (c t)"),
            )

        def unit(uu):
            r, u = divmod(uu, 8)
            f, cb = divmod(u, 4)
            return r, f, cb, 2 * (r // 2) + f

        def one_pass(acc, t_idx, j, r):
            nc.tensor.matmul_mx(
                out=acc[:],
                lhsT=wqt[t_idx][:, 128 * j : 128 * j + 128].bitcast(FP8X4),
                lhsT_scale=wst[t_idx][:, 128 * j : 128 * j + 128],
                rhs=aqt[r][:].bitcast(FP8X4),
                rhs_scale=ast[r][:],
                start=True,
                stop=True,
            )

        def mx_gate(uu):
            if uu < 8 * N_ROUNDS:
                r, f, cb, t_idx = unit(uu)
                rbs[uu] = psr.tile([P, 512], F32, name="rb", tag="rb")
                one_pass(rbs[uu], t_idx, 4 + cb, r)

        def mx_value(uu):
            if uu < 8 * N_ROUNDS:
                r, f, cb, t_idx = unit(uu)
                lbs[uu] = psl.tile([P, 512], F32, name="lb", tag="lb")
                one_pass(lbs[uu], t_idx, cb, r)

        def sig(uu):
            if uu >= 8 * N_ROUNDS:
                return
            r, f, cb, t_idx = unit(uu)
            col = 8 * t_idx + 4 + cb
            sts[uu] = sp.tile([P, 512], F32, name="s", tag="s")
            nc.scalar.activation(
                out=sts[uu][:], in_=rbs[uu][:], func=ACT.Sigmoid, bias=bias_sb[:, col : col + 1], scale=1.0
            )

        def stt(uu):
            r, f, cb, t_idx = unit(uu)
            col = 8 * t_idx + cb
            if f == 0:
                if cb == 0:
                    g0t[r] = g0p.tile([P, 4, 512], F32, name="g0", tag="g0")
                dst = g0t[r][:, cb, :]
            else:
                g1t[(r, cb)] = g1p.tile([P, 512], F32, name="g1", tag="g1")
                dst = g1t[(r, cb)][:]
            nc.vector.scalar_tensor_tensor(
                out=dst,
                in0=lbs[uu][:],
                scalar=bias_sb[:, col : col + 1],
                in1=sts[uu][:],
                op0=ALU.add,
                op1=ALU.mult,
            )

        def vmax(r, cb):
            nc.vector.tensor_tensor(
                out=g0t[r][:, cb, :], in0=g0t[r][:, cb, :], in1=g1t[(r, cb)][:], op=ALU.max
            )

        def out_t(r, nt, big):
            if big:
                ob = psl.tile([P, 512], F32, name="ob2", tag="lb")
            else:
                ob = pst.tile([P, 512], F32, name="ob", tag="tp")
            for cb in range(4):
                nc.tensor.transpose(
                    ob[:, 128 * cb : 128 * cb + 128], g0t[r][:, cb, 128 * nt : 128 * nt + 128], ident[:]
                )
            obs[(r, nt)] = ob

        def out_copy(r, nt, on_vector):
            if nt == 0:
                ots[r] = op.tile([P, 4, 512], F32, name="o", tag="o")
            if on_vector:
                nc.vector.tensor_copy(out=ots[r][:, nt, :], in_=obs[(r, nt)][:])
            else:
                nc.scalar.copy(out=ots[r][:, nt, :], in_=obs[(r, nt)][:])

        def out_t_cb(cb):
            if cb < 2:
                ob = pst.tile([P, 4, P], F32, name="oc", tag="tp")
            else:
                ob = psr.tile([P, 4, P], F32, name="oc", tag="rb")
            for nt in range(4):
                nc.tensor.transpose(ob[:, nt, :], g0t[7][:, cb, P * nt : P * nt + P], ident[:])
            obs[cb] = ob

        def out_copy_cb(cb, n0, n1, on_vector):
            half, part = divmod(cb, 2)
            if part == 0 and n0 == 0:
                ots[(7, half)] = op.tile([P, 4, 256], F32, name="oh", tag="oh")
            dst = ots[(7, half)][:, n0:n1, P * part : P * part + P]
            src = obs[cb][:, n0:n1, :]
            if on_vector:
                nc.vector.tensor_copy(out=dst, in_=src)
            else:
                nc.scalar.copy(out=dst, in_=src)

        def store_half(half):
            nc.sync.dma_start(
                out=out[1, 3].rearrange("(p nt) c -> p nt c", nt=4)[:, :, 256 * half : 256 * half + 256],
                in_=ots[(7, half)][:],
            )

        def store(r, n0, n1):
            w, i = divmod(r, 2)
            nc.sync.dma_start(
                out=out[i, w].rearrange("(p nt) c -> p nt c", nt=4)[:, n0:n1, :], in_=ots[r][:, n0:n1, :]
            )


        regroup(0, 512, 832, True)
        regroup(0, 832, 1024, False)
        regroup(0, 0, 320, True)
        regroup(0, 320, 512, False)
        w_q(0, 512, 1024)
        agg_t(0, 0)
        agg_t(0, 1)
        w_q(0, 0, 512)
        agg_copy(0, 0)
        agg_copy(0, 1)
        bt = psl.tile([P, 512], F32, name="bt", tag="lb")
        nc.tensor.transpose(bt[:, 0:128], bf32[:], ident[:])
        nc.vector.tensor_copy(out=bias_sb[:], in_=bt[:, 0:64])
        agg_q(0)
        regroup(1, 0, 768, True)
        regroup(1, 768, 1024, False)
        for k in range(LEAD + 2):
            mx_gate(k)
            if k < 3:
                mx_value(k)
            if k < LEAD:
                sig(k)

        for r in range(N_ROUNDS):
            cv, end = (608, 1024) if r < 2 else (CV, 1024 - GC)
            first = 4 if r < N_ROUNDS - 1 else 2
            for u in range(8):
                uu = 8 * r + u
                if u == 0 and r >= 1:
                    vmax(r - 1, 3)
                if u == 0 and 1 <= r < 7:
                    w_q(r + 1)
                    if r == 1:
                        regroup(3, cv, (cv + end) // 2, False)
                    if r + 3 < 8:
                        regroup_g(r + 3)
                if u == 4 and r + 1 < N_ROUNDS:
                    agg_q(r + 1)
                mx_value(uu + 3)
                if u == 0 and r + 1 < N_ROUNDS:
                    agg_t(r + 1, 0)
                    agg_t(r + 1, 1)
                if r >= 1:
                    if u == first - 1:
                        out_t(r - 1, 0, False)
                        out_t(r - 1, 1, False)
                    if u == first + 1:
                        out_t(r - 1, 2, False)
                    if u == first + 2:
                        out_t(r - 1, 3, False)
                sig(uu + LEAD)
                if uu > 0:
                    mx_gate(uu + LEAD + 2)
                if u == 0 and r + 2 < 8 and r != 1:
                    regroup(r + 2, cv, (cv + end) // 2, False)
                if u in (1, 2) and r + 1 < N_ROUNDS:
                    agg_copy(r + 1, u - 1)
                if u == 3 and r + 2 < 8:
                    regroup(r + 2, (cv + end) // 2, end, False)
                if first <= u < first + 4 and r >= 1:
                    out_copy(r - 1, u - first, False)
                    if u == first + 1:
                        store(r - 1, 0, 2)
                    if u == first + 3:
                        store(r - 1, 2, 4)
                stt(uu)
                if uu == 0:
                    w_q(1)
                    mx_gate(LEAD + 2)
                if u == (2 if r == 0 else 3) and r + 2 < 8:
                    regroup(r + 2, 0, cv // 2, True)
                if u == (3 if r == 0 else 4) and r + 2 < 8:
                    regroup(r + 2, cv // 2, cv, True)
                if u >= 5:
                    vmax(r, u - 5)
                    if r == N_ROUNDS - 1:
                        out_t_cb(u - 5)
                        if u > 5:
                            out_copy_cb(u - 6, 0, 4, False)

        vmax(7, 3)
        store_half(0)
        out_t_cb(3)
        out_copy_cb(2, 0, 2, True)
        out_copy_cb(2, 2, 4, False)
        out_copy_cb(3, 0, 2, True)
        out_copy_cb(3, 2, 4, False)
        store_half(1)
